import numpy as np
import ml_dtypes


def mxq(x, axis, fmt="e4m3"):
    dtype, down = {"e4m3": (ml_dtypes.float8_e4m3fn, 7), "e5m2": (ml_dtypes.float8_e5m2, 14)}[fmt]
    v = np.moveaxis(np.asarray(x, np.float32).astype(ml_dtypes.bfloat16).astype(np.float64), axis, -1)
    blocks = v.reshape(v.shape[:-1] + (-1, 32))
    amax = np.abs(blocks).max(-1, keepdims=True)
    byte = np.maximum(np.where(amax > 0, np.frexp(amax)[1] - 1 + 127, 0) - down, 1)
    scale = np.exp2(byte - 127.0)
    codes = (blocks / scale).astype(np.float32).astype(dtype).astype(np.float64)
    return np.moveaxis((codes * scale).reshape(v.shape), -1, axis)


WIDE = False


def mx_kscale(k):
    if not WIDE:
        return np.ones(k)
    levels = np.array([10, -10, 5, -5, 0])
    if k % 512:
        return np.exp2(np.random.permutation(np.resize(levels, k // 32))).repeat(32)
    a = np.empty((k // 512, 16))
    for p in range(k // 512):
        a[p, :8] = np.random.permutation(np.resize(levels, 8))
        for g in range(8):
            far = levels[np.abs(levels - a[p, g]) >= 10]
            a[p, g + 8] = far[np.random.randint(len(far))]
    return np.exp2(a.ravel()).repeat(32)


BF16 = ml_dtypes.bfloat16


def bf(x):
    return np.asarray(x, np.float32).astype(BF16)


def f64(x):
    return np.asarray(x).astype(np.float64)


B, N, IN_DIM, UNITS, K = 2, 1024, 128, 128, 3
F = IN_DIM + UNITS


def setup_inputs():
    s = mx_kscale(N)
    adj = np.random.standard_normal((N, N)) * 0.5 / np.sqrt(N) * s[None, :] / s[:, None]
    x0 = np.random.standard_normal((B, N, F)) / s[None, :, None]
    return {"adj": bf(adj), "x0": bf(x0)}


def reference(adj, x0):
    aq = mxq(f64(adj), 1, "e4m3")
    x0 = f64(x0)
    x1 = aq @ mxq(x0, 1, "e4m3")
    x2 = 2.0 * (aq @ mxq(x1, 1, "e4m3")) - x0
    return x1, x2

@@ -1,0 +1,194 @@
+import concourse.mybir as mybir
+from concourse.masks import make_identity
+
+BF16 = mybir.dt.bfloat16
+F32 = mybir.dt.float32
+U32 = mybir.dt.uint32
+U8 = mybir.dt.uint8
+FP8X4 = mybir.dt.float8_e4m3fn_x4
+
+P = 128
+PACK = 4
+PAIR = 2
+NODES = 1024
+BATCH = 2
+FEATURES = 256
+PASSES = NODES // (P * PACK)
+CHUNKS = NODES // (P * PAIR)
+CHUNKS_PER_PASS = CHUNKS // PASSES
+WORDS = NODES // PAIR
+
+FLOPS = 2 * 2 * NODES * NODES * BATCH * FEATURES
+RUN = 4
+WARM_UP = 8
+
+
+def tile_gts_gcgrucell_pa_kernel(tc, adj, x0, out_0, out_1):
+    nc = tc.nc
+    with tc.tile_pool(name="keep", bufs=1) as keep, tc.psum_pool(name="psum", bufs=8) as psum:
+        identity = keep.tile([P, P], F32)
+        zeros = keep.tile([P, PACK * P], BF16)
+        x0_rows, x1_rows, x2_rows = [], [], []
+        x0_grouped, x0_codes, x0_scales = [], [], []
+        x1_grouped, x1_codes, x1_scales = [], [], []
+        for b in range(BATCH):
+            x0_rows.append(keep.tile([P, CHUNKS, PAIR, FEATURES], BF16, name="x0_rows%d" % b))
+            x1_rows.append(keep.tile([P, CHUNKS, PAIR, FEATURES], F32, name="x1_rows%d" % b))
+            x2_rows.append(keep.tile([P, CHUNKS, PAIR, FEATURES], F32, name="x2_rows%d" % b))
+            grouped_shape = [P, PASSES, FEATURES, PACK]
+            x0_grouped.append(keep.tile(grouped_shape, BF16, name="x0_grouped%d" % b, align_bytes=64))
+            x1_grouped.append(keep.tile(grouped_shape, BF16, name="x1_grouped%d" % b, align_bytes=64))
+            x0_codes.append(keep.tile([P, PASSES, FEATURES], U32, name="x0_codes%d" % b, align_bytes=64))
+            x0_scales.append(keep.tile([P, PASSES, FEATURES], U8, name="x0_scales%d" % b, align_bytes=64))
+            x1_codes.append(keep.tile([P, PASSES, FEATURES], U32, name="x1_codes%d" % b, align_bytes=64))
+            x1_scales.append(keep.tile([P, PASSES, FEATURES], U8, name="x1_scales%d" % b, align_bytes=64))
+        adj_rows, adj_grouped, adj_codes, adj_scales = [], [], [], []
+        for c in range(CHUNKS):
+            adj_rows.append(keep.tile([P, PAIR * NODES], BF16, name="adj_rows%d" % c))
+            adj_grouped.append(
+                keep.tile([P, PAIR, PASSES * P * PACK], BF16, name="adj_grouped%d" % c, align_bytes=64)
+            )
+            adj_codes.append(keep.tile([P, PAIR, PASSES, P], U32, name="adj_codes%d" % c, align_bytes=64))
+            adj_scales.append(keep.tile([P, PAIR, PASSES, P], U8, name="adj_scales%d" % c, align_bytes=64))
+
+        def load_x0(b, g):
+            chunks = slice(g * CHUNKS_PER_PASS, (g + 1) * CHUNKS_PER_PASS)
+            nodes = slice(g * P * PACK, (g + 1) * P * PACK)
+            nc.sync.dma_start(
+                out=x0_rows[b][:, chunks].rearrange("p h e f -> p (h e f)"),
+                in_=x0[b, nodes, :].rearrange("(p t) f -> p (t f)", t=PACK),
+            )
+
+        def chunk_rows(array, c):
+            g, h = divmod(c, CHUNKS_PER_PASS)
+            nodes = slice(g * P * PACK, (g + 1) * P * PACK)
+            return array[nodes, :].rearrange("(p h e) k -> h p (e k)", h=CHUNKS_PER_PASS, e=PAIR)[h]
+
+        def load_adj(c):
+            nc.sync.dma_start(out=adj_rows[c][:], in_=chunk_rows(adj, c))
+
+        def store(out, rows, b, c):
+            nc.sync.dma_start(
+                out=chunk_rows(out[b], c),
+                in_=rows[b][:, c].rearrange("p e f -> p (e f)"),
+            )
+
+        def regroup(grouped, rows, b, g):
+            chunks = slice(g * CHUNKS_PER_PASS, (g + 1) * CHUNKS_PER_PASS)
+            nc.vector.tensor_copy(
+                out=grouped[b][:, g].rearrange("p (n i) t -> p n t i", i=RUN),
+                in_=rows[b][:, chunks].rearrange("p u e (n i) -> p n (u e) i", i=RUN),
+            )
+
+        def quantise(grouped, codes, scales):
+            nc.vector.quantize_mx(out=codes.bitcast(FP8X4), scales=scales, in_=grouped)
+
+        def quantise_x0(b):
+            quantise(
+                x0_grouped[b][:].rearrange("p g f t -> p (g f t)"),
+                x0_codes[b][:].rearrange("p g f -> p (g f)"),
+                x0_scales[b][:].rearrange("p g f -> p (g f)"),
+            )
+
+        def transpose_adj(c, e):
+            words = adj_rows[c][:].bitcast(F32)
+            flipped = psum.tile([P, CHUNKS, P], F32, tag="bank")
+            for j in range(CHUNKS):
+                g, h = divmod(j, CHUNKS_PER_PASS)
+                start = e * WORDS + g * P * CHUNKS_PER_PASS
+                stop = start + P * CHUNKS_PER_PASS
+                nc.tensor.transpose(flipped[:, j, :], words[:, start + h : stop : CHUNKS_PER_PASS], identity[:])
+            nc.scalar.copy(
+                out=adj_grouped[c][:, e].bitcast(F32).rearrange(
+                    "p (g r u) -> p g r u", g=PASSES, u=CHUNKS_PER_PASS
+                ),
+                in_=flipped[:].rearrange("p (g u) r -> p g r u", u=CHUNKS_PER_PASS),
+            )
+            quantise(
+                adj_grouped[c][:, e],
+                adj_codes[c][:, e].rearrange("p g r -> p (g r)"),
+                adj_scales[c][:, e].rearrange("p g r -> p (g r)"),
+            )
+
+        def multiply_zeros(unused):
+            nc.tensor.matmul(out=unused[:], lhsT=zeros[:, :P], rhs=zeros[:], start=True, stop=True)
+
+        def multiply(c, codes, scales):
+            product = psum.tile([P, PAIR, FEATURES], F32, tag="bank")
+            for e in range(PAIR):
+                for g in range(PASSES):
+                    nc.tensor.matmul_mx(
+                        out=product[:, e, :],
+                        lhsT=adj_codes[c][:, e, g, :].bitcast(FP8X4),
+                        lhsT_scale=adj_scales[c][:, e, g, :],
+                        rhs=codes[:, g, :].bitcast(FP8X4),
+                        rhs_scale=scales[:, g, :],
+                        start=(g == 0),
+                        stop=(g == PASSES - 1),
+                    )
+            return product
+
+        def first_product(b, c):
+            product = multiply(c, x0_codes[b], x0_scales[b])
+            nc.scalar.copy(out=x1_rows[b][:, c], in_=product[:])
+            store(out_0, x1_rows, b, c)
+
+        def quantise_x1(b, g):
+            quantise(x1_grouped[b][:, g].rearrange("p f t -> p (f t)"), x1_codes[b][:, g], x1_scales[b][:, g])
+
+        def second_product(b, c):
+            product = multiply(c, x1_codes[b], x1_scales[b])
+            nc.vector.scalar_tensor_tensor(
+                out=x2_rows[b][:, c],
+                in0=product[:],
+                scalar=2.0,
+                in1=x0_rows[b][:, c],
+                op0=mybir.AluOpType.mult,
+                op1=mybir.AluOpType.subtract,
+            )
+            store(out_1, x2_rows, b, c)
+
+        with tc.manual_schedule():
+            for g in range(PASSES):
+                load_x0(0, g)
+            for c in range(CHUNKS):
+                load_adj(c)
+            for g in range(PASSES):
+                load_x0(1, g)
+            make_identity(nc, identity[:])
+
+            nc.vector.memset(zeros[:], 0.0)
+            unused = psum.tile([P, PACK * P], F32, tag="bank")
+            for i in range(WARM_UP):
+                multiply_zeros(unused)
+
+            for g in range(PASSES):
+                regroup(x0_grouped, x0_rows, 0, g)
+            quantise_x0(0)
+            for c in range(CHUNKS - 1):
+                for e in range(PAIR):
+                    transpose_adj(c, e)
+                multiply_zeros(unused)
+            for g, e in zip(range(PASSES), range(PAIR)):
+                regroup(x0_grouped, x0_rows, 1, g)
+                transpose_adj(CHUNKS - 1, e)
+            quantise_x0(1)
+
+            for c in range(CHUNKS):
+                first_product(0, c)
+                if c % CHUNKS_PER_PASS == CHUNKS_PER_PASS - 1:
+                    regroup(x1_grouped, x1_rows, 0, c // CHUNKS_PER_PASS)
+                    quantise_x1(0, c // CHUNKS_PER_PASS)
+            for c in range(CHUNKS_PER_PASS):
+                first_product(1, c)
+            regroup(x1_grouped, x1_rows, 1, 0)
+            quantise_x1(1, 0)
+            for c in range(CHUNKS_PER_PASS, CHUNKS):
+                first_product(1, c)
+            regroup(x1_grouped, x1_rows, 1, 1)
+            second_product(0, 0)
+            quantise_x1(1, 1)
+            for c in range(1, CHUNKS):
+                second_product(0, c)
+            for c in range(CHUNKS):
+                second_product(1, c)

@@ -168,7 +168,6 @@ def tile_gts_gcgrucell_pa_kernel(tc, adj, x0, out_0, out_1):
             for c in range(CHUNKS - 1):
                 for e in range(PAIR):
                     transpose_adj(c, e)
-                multiply_zeros(unused)
             for g, e in zip(range(PASSES), range(PAIR)):
                 regroup(x0_grouped, x0_rows, 1, g)
                 transpose_adj(CHUNKS - 1, e)

@@ -28,13 +28,14 @@ def tile_gts_gcgrucell_pa_kernel(tc, adj, x0, out_0, out_1):
     with tc.tile_pool(name="keep", bufs=1) as keep, tc.psum_pool(name="psum", bufs=8) as psum:
         identity = keep.tile([P, P], F32)
         zeros = keep.tile([P, PACK * P], BF16)
-        x0_rows, x1_rows, x2_rows = [], [], []
+        x0_rows, x1_rows, x2_rows, doubled = [], [], [], []
         x0_grouped, x0_codes, x0_scales = [], [], []
         x1_grouped, x1_codes, x1_scales = [], [], []
         for b in range(BATCH):
             x0_rows.append(keep.tile([P, CHUNKS, PAIR, FEATURES], BF16, name="x0_rows%d" % b))
             x1_rows.append(keep.tile([P, CHUNKS, PAIR, FEATURES], F32, name="x1_rows%d" % b))
             x2_rows.append(keep.tile([P, CHUNKS, PAIR, FEATURES], F32, name="x2_rows%d" % b))
+            doubled.append(keep.tile([P, CHUNKS, PAIR, FEATURES], F32, name="doubled%d" % b))
             grouped_shape = [P, PASSES, FEATURES, PACK]
             x0_grouped.append(keep.tile(grouped_shape, BF16, name="x0_grouped%d" % b, align_bytes=64))
             x1_grouped.append(keep.tile(grouped_shape, BF16, name="x1_grouped%d" % b, align_bytes=64))
@@ -148,6 +149,13 @@ def tile_gts_gcgrucell_pa_kernel(tc, adj, x0, out_0, out_1):
             )
             store(out_1, x2_rows, b, c)
 
+        def second_product_shared(b, c):
+            product = multiply(c, x1_codes[b], x1_scales[b])
+            nc.scalar.mul(out=doubled[b][:, c], in_=product[:], mul=2.0)
+            nc.gpsimd.tensor_tensor(
+                out=x2_rows[b][:, c], in0=doubled[b][:, c], in1=x0_rows[b][:, c], op=mybir.AluOpType.subtract
+            )
+
         with tc.manual_schedule():
             for g in range(PASSES):
                 load_x0(0, g)
@@ -187,7 +195,12 @@ def tile_gts_gcgrucell_pa_kernel(tc, adj, x0, out_0, out_1):
             regroup(x1_grouped, x1_rows, 1, 1)
             second_product(0, 0)
             quantise_x1(1, 1)
-            for c in range(1, CHUNKS):
-                second_product(0, c)
-            for c in range(CHUNKS):
-                second_product(1, c)
+            second_product_shared(0, 1)
+            second_product(0, 2)
+            second_product(0, 3)
+            store(out_1, x2_rows, 0, 1)
+            second_product_shared(1, 0)
+            second_product(1, 1)
+            second_product(1, 2)
+            store(out_1, x2_rows, 1, 0)
+            second_product(1, 3)

@@ -27,15 +27,15 @@ def tile_gts_gcgrucell_pa_kernel(tc, adj, x0, out_0, out_1):
     nc = tc.nc
     with tc.tile_pool(name="keep", bufs=1) as keep, tc.psum_pool(name="psum", bufs=8) as psum:
         identity = keep.tile([P, P], F32)
+        doubled = keep.tile([P, PAIR, FEATURES], F32)
         zeros = keep.tile([P, PACK * P], BF16)
-        x0_rows, x1_rows, x2_rows, doubled = [], [], [], []
+        x0_rows, x1_rows, x2_rows = [], [], []
         x0_grouped, x0_codes, x0_scales = [], [], []
         x1_grouped, x1_codes, x1_scales = [], [], []
         for b in range(BATCH):
             x0_rows.append(keep.tile([P, CHUNKS, PAIR, FEATURES], BF16, name="x0_rows%d" % b))
             x1_rows.append(keep.tile([P, CHUNKS, PAIR, FEATURES], F32, name="x1_rows%d" % b))
             x2_rows.append(keep.tile([P, CHUNKS, PAIR, FEATURES], F32, name="x2_rows%d" % b))
-            doubled.append(keep.tile([P, CHUNKS, PAIR, FEATURES], F32, name="doubled%d" % b))
             grouped_shape = [P, PASSES, FEATURES, PACK]
             x0_grouped.append(keep.tile(grouped_shape, BF16, name="x0_grouped%d" % b, align_bytes=64))
             x1_grouped.append(keep.tile(grouped_shape, BF16, name="x1_grouped%d" % b, align_bytes=64))
@@ -84,12 +84,8 @@ def tile_gts_gcgrucell_pa_kernel(tc, adj, x0, out_0, out_1):
         def quantise(grouped, codes, scales):
             nc.vector.quantize_mx(out=codes.bitcast(FP8X4), scales=scales, in_=grouped)
 
-        def quantise_x0(b):
-            quantise(
-                x0_grouped[b][:].rearrange("p g f t -> p (g f t)"),
-                x0_codes[b][:].rearrange("p g f -> p (g f)"),
-                x0_scales[b][:].rearrange("p g f -> p (g f)"),
-            )
+        def quantise_x0(b, g):
+            quantise(x0_grouped[b][:, g].rearrange("p f t -> p (f t)"), x0_codes[b][:, g], x0_scales[b][:, g])
 
         def transpose_adj(c, e):
             words = adj_rows[c][:].bitcast(F32)
@@ -99,12 +95,17 @@ def tile_gts_gcgrucell_pa_kernel(tc, adj, x0, out_0, out_1):
                 start = e * WORDS + g * P * CHUNKS_PER_PASS
                 stop = start + P * CHUNKS_PER_PASS
                 nc.tensor.transpose(flipped[:, j, :], words[:, start + h : stop : CHUNKS_PER_PASS], identity[:])
+            return flipped
+
+        def copy_adj(c, e, flipped):
             nc.scalar.copy(
                 out=adj_grouped[c][:, e].bitcast(F32).rearrange(
                     "p (g r u) -> p g r u", g=PASSES, u=CHUNKS_PER_PASS
                 ),
                 in_=flipped[:].rearrange("p (g u) r -> p g r u", u=CHUNKS_PER_PASS),
             )
+
+        def quantise_adj(c, e):
             quantise(
                 adj_grouped[c][:, e],
                 adj_codes[c][:, e].rearrange("p g r -> p (g r)"),
@@ -151,9 +152,9 @@ def tile_gts_gcgrucell_pa_kernel(tc, adj, x0, out_0, out_1):
 
         def second_product_shared(b, c):
             product = multiply(c, x1_codes[b], x1_scales[b])
-            nc.scalar.mul(out=doubled[b][:, c], in_=product[:], mul=2.0)
+            nc.scalar.mul(out=doubled[:], in_=product[:], mul=2.0)
             nc.gpsimd.tensor_tensor(
-                out=x2_rows[b][:, c], in0=doubled[b][:, c], in1=x0_rows[b][:, c], op=mybir.AluOpType.subtract
+                out=x2_rows[b][:, c], in0=doubled[:], in1=x0_rows[b][:, c], op=mybir.AluOpType.subtract
             )
 
         with tc.manual_schedule():
@@ -172,35 +173,35 @@ def tile_gts_gcgrucell_pa_kernel(tc, adj, x0, out_0, out_1):
 
             for g in range(PASSES):
                 regroup(x0_grouped, x0_rows, 0, g)
-            quantise_x0(0)
-            for c in range(CHUNKS - 1):
+                quantise_x0(0, g)
+            for c in range(CHUNKS):
                 for e in range(PAIR):
-                    transpose_adj(c, e)
-            for g, e in zip(range(PASSES), range(PAIR)):
-                regroup(x0_grouped, x0_rows, 1, g)
-                transpose_adj(CHUNKS - 1, e)
-            quantise_x0(1)
+                    copy_adj(c, e, transpose_adj(c, e))
+                quantise_adj(c, 0)
+                if c >= CHUNKS - PASSES:
+                    regroup(x0_grouped, x0_rows, 1, c - (CHUNKS - PASSES))
+                quantise_adj(c, 1)
+            for g in range(PASSES):
+                quantise_x0(1, g)
 
             for c in range(CHUNKS):
                 first_product(0, c)
-                if c % CHUNKS_PER_PASS == CHUNKS_PER_PASS - 1:
-                    regroup(x1_grouped, x1_rows, 0, c // CHUNKS_PER_PASS)
-                    quantise_x1(0, c // CHUNKS_PER_PASS)
+            for g in range(PASSES):
+                regroup(x1_grouped, x1_rows, 0, g)
+            for g in range(PASSES):
+                quantise_x1(0, g)
             for c in range(CHUNKS_PER_PASS):
                 first_product(1, c)
             regroup(x1_grouped, x1_rows, 1, 0)
             quantise_x1(1, 0)
             for c in range(CHUNKS_PER_PASS, CHUNKS):
                 first_product(1, c)
-            regroup(x1_grouped, x1_rows, 1, 1)
             second_product(0, 0)
-            quantise_x1(1, 1)
+            regroup(x1_grouped, x1_rows, 1, 1)
             second_product_shared(0, 1)
             second_product(0, 2)
-            second_product(0, 3)
             store(out_1, x2_rows, 0, 1)
-            second_product_shared(1, 0)
-            second_product(1, 1)
-            second_product(1, 2)
-            store(out_1, x2_rows, 1, 0)
-            second_product(1, 3)
+            quantise_x1(1, 1)
+            second_product(0, 3)
+            for c in range(CHUNKS):
+                second_product(1, c)

@@ -27,7 +27,6 @@ def tile_gts_gcgrucell_pa_kernel(tc, adj, x0, out_0, out_1):
     nc = tc.nc
     with tc.tile_pool(name="keep", bufs=1) as keep, tc.psum_pool(name="psum", bufs=8) as psum:
         identity = keep.tile([P, P], F32)
-        doubled = keep.tile([P, PAIR, FEATURES], F32)
         zeros = keep.tile([P, PACK * P], BF16)
         x0_rows, x1_rows, x2_rows = [], [], []
         x0_grouped, x0_codes, x0_scales = [], [], []
@@ -150,13 +149,6 @@ def tile_gts_gcgrucell_pa_kernel(tc, adj, x0, out_0, out_1):
             )
             store(out_1, x2_rows, b, c)
 
-        def second_product_shared(b, c):
-            product = multiply(c, x1_codes[b], x1_scales[b])
-            nc.scalar.mul(out=doubled[:], in_=product[:], mul=2.0)
-            nc.gpsimd.tensor_tensor(
-                out=x2_rows[b][:, c], in0=doubled[:], in1=x0_rows[b][:, c], op=mybir.AluOpType.subtract
-            )
-
         with tc.manual_schedule():
             for g in range(PASSES):
                 load_x0(0, g)
@@ -198,10 +190,9 @@ def tile_gts_gcgrucell_pa_kernel(tc, adj, x0, out_0, out_1):
                 first_product(1, c)
             second_product(0, 0)
             regroup(x1_grouped, x1_rows, 1, 1)
-            second_product_shared(0, 1)
-            second_product(0, 2)
-            store(out_1, x2_rows, 0, 1)
+            second_product(0, 1)
             quantise_x1(1, 1)
-            second_product(0, 3)
+            for c in range(CHUNKS_PER_PASS, CHUNKS):
+                second_product(0, c)
             for c in range(CHUNKS):
                 second_product(1, c)

@@ -73,9 +73,9 @@ def tile_gts_gcgrucell_pa_kernel(tc, adj, x0, out_0, out_1):
                 in_=rows[b][:, c].rearrange("p e f -> p (e f)"),
             )
 
-        def regroup(grouped, rows, b, g):
+        def regroup(copy, grouped, rows, b, g):
             chunks = slice(g * CHUNKS_PER_PASS, (g + 1) * CHUNKS_PER_PASS)
-            nc.vector.tensor_copy(
+            copy(
                 out=grouped[b][:, g].rearrange("p (n i) t -> p n t i", i=RUN),
                 in_=rows[b][:, chunks].rearrange("p u e (n i) -> p n (u e) i", i=RUN),
             )
@@ -164,14 +164,14 @@ def tile_gts_gcgrucell_pa_kernel(tc, adj, x0, out_0, out_1):
                 multiply_zeros(unused)
 
             for g in range(PASSES):
-                regroup(x0_grouped, x0_rows, 0, g)
+                regroup(nc.vector.tensor_copy, x0_grouped, x0_rows, 0, g)
                 quantise_x0(0, g)
             for c in range(CHUNKS):
                 for e in range(PAIR):
                     copy_adj(c, e, transpose_adj(c, e))
                 quantise_adj(c, 0)
                 if c >= CHUNKS - PASSES:
-                    regroup(x0_grouped, x0_rows, 1, c - (CHUNKS - PASSES))
+                    regroup(nc.vector.tensor_copy, x0_grouped, x0_rows, 1, c - (CHUNKS - PASSES))
                 quantise_adj(c, 1)
             for g in range(PASSES):
                 quantise_x0(1, g)
@@ -179,20 +179,20 @@ def tile_gts_gcgrucell_pa_kernel(tc, adj, x0, out_0, out_1):
             for c in range(CHUNKS):
                 first_product(0, c)
             for g in range(PASSES):
-                regroup(x1_grouped, x1_rows, 0, g)
+                regroup(nc.vector.tensor_copy, x1_grouped, x1_rows, 0, g)
             for g in range(PASSES):
                 quantise_x1(0, g)
             for c in range(CHUNKS_PER_PASS):
                 first_product(1, c)
-            regroup(x1_grouped, x1_rows, 1, 0)
-            quantise_x1(1, 0)
+            regroup(nc.vector.tensor_copy, x1_grouped, x1_rows, 1, 0)
             for c in range(CHUNKS_PER_PASS, CHUNKS):
                 first_product(1, c)
+            regroup(nc.scalar.copy, x1_grouped, x1_rows, 1, 1)
             second_product(0, 0)
-            regroup(x1_grouped, x1_rows, 1, 1)
+            quantise_x1(1, 0)
             second_product(0, 1)
             quantise_x1(1, 1)
-            for c in range(CHUNKS_PER_PASS, CHUNKS):
+            for c in range(2, CHUNKS):
                 second_product(0, c)
             for c in range(CHUNKS):
                 second_product(1, c)

@@ -67,8 +67,8 @@ def tile_gts_gcgrucell_pa_kernel(tc, adj, x0, out_0, out_1):
         def load_adj(c):
             nc.sync.dma_start(out=adj_rows[c][:], in_=chunk_rows(adj, c))
 
-        def store(out, rows, b, c):
-            nc.sync.dma_start(
+        def store(queue, out, rows, b, c):
+            queue.dma_start(
                 out=chunk_rows(out[b], c),
                 in_=rows[b][:, c].rearrange("p e f -> p (e f)"),
             )
@@ -132,7 +132,7 @@ def tile_gts_gcgrucell_pa_kernel(tc, adj, x0, out_0, out_1):
         def first_product(b, c):
             product = multiply(c, x0_codes[b], x0_scales[b])
             nc.scalar.copy(out=x1_rows[b][:, c], in_=product[:])
-            store(out_0, x1_rows, b, c)
+            store(nc.sync, out_0, x1_rows, b, c)
 
         def quantise_x1(b, g):
             quantise(x1_grouped[b][:, g].rearrange("p f t -> p (f t)"), x1_codes[b][:, g], x1_scales[b][:, g])
@@ -147,7 +147,7 @@ def tile_gts_gcgrucell_pa_kernel(tc, adj, x0, out_0, out_1):
                 op0=mybir.AluOpType.mult,
                 op1=mybir.AluOpType.subtract,
             )
-            store(out_1, x2_rows, b, c)
+            store((nc.sync, nc.scalar)[c % 2], out_1, x2_rows, b, c)
 
         with tc.manual_schedule():
             for g in range(PASSES):

import concourse.mybir as mybir
from concourse.masks import make_identity

BF16 = mybir.dt.bfloat16
F32 = mybir.dt.float32
U32 = mybir.dt.uint32
U8 = mybir.dt.uint8
FP8X4 = mybir.dt.float8_e4m3fn_x4

P = 128
PACK = 4
PAIR = 2
NODES = 1024
BATCH = 2
FEATURES = 256
PASSES = NODES // (P * PACK)
CHUNKS = NODES // (P * PAIR)
CHUNKS_PER_PASS = CHUNKS // PASSES
WORDS = NODES // PAIR

FLOPS = 2 * 2 * NODES * NODES * BATCH * FEATURES
RUN = 4
WARM_UP = 8


def tile_gts_gcgrucell_pa_kernel(tc, adj, x0, out_0, out_1):
    nc = tc.nc
    with tc.tile_pool(name="keep", bufs=1) as keep, tc.psum_pool(name="psum", bufs=8) as psum:
        identity = keep.tile([P, P], F32)
        zeros = keep.tile([P, PACK * P], BF16)
        x0_rows, x1_rows, x2_rows = [], [], []
        x0_grouped, x0_codes, x0_scales = [], [], []
        x1_grouped, x1_codes, x1_scales = [], [], []
        for b in range(BATCH):
            x0_rows.append(keep.tile([P, CHUNKS, PAIR, FEATURES], BF16, name="x0_rows%d" % b))
            x1_rows.append(keep.tile([P, CHUNKS, PAIR, FEATURES], F32, name="x1_rows%d" % b))
            x2_rows.append(keep.tile([P, CHUNKS, PAIR, FEATURES], F32, name="x2_rows%d" % b))
            grouped_shape = [P, PASSES, FEATURES, PACK]
            x0_grouped.append(keep.tile(grouped_shape, BF16, name="x0_grouped%d" % b, align_bytes=64))
            x1_grouped.append(keep.tile(grouped_shape, BF16, name="x1_grouped%d" % b, align_bytes=64))
            x0_codes.append(keep.tile([P, PASSES, FEATURES], U32, name="x0_codes%d" % b, align_bytes=64))
            x0_scales.append(keep.tile([P, PASSES, FEATURES], U8, name="x0_scales%d" % b, align_bytes=64))
            x1_codes.append(keep.tile([P, PASSES, FEATURES], U32, name="x1_codes%d" % b, align_bytes=64))
            x1_scales.append(keep.tile([P, PASSES, FEATURES], U8, name="x1_scales%d" % b, align_bytes=64))
        adj_rows, adj_grouped, adj_codes, adj_scales = [], [], [], []
        for c in range(CHUNKS):
            adj_rows.append(keep.tile([P, PAIR * NODES], BF16, name="adj_rows%d" % c))
            adj_grouped.append(
                keep.tile([P, PAIR, PASSES * P * PACK], BF16, name="adj_grouped%d" % c, align_bytes=64)
            )
            adj_codes.append(keep.tile([P, PAIR, PASSES, P], U32, name="adj_codes%d" % c, align_bytes=64))
            adj_scales.append(keep.tile([P, PAIR, PASSES, P], U8, name="adj_scales%d" % c, align_bytes=64))

        def load_x0(b, g):
            chunks = slice(g * CHUNKS_PER_PASS, (g + 1) * CHUNKS_PER_PASS)
            nodes = slice(g * P * PACK, (g + 1) * P * PACK)
            nc.sync.dma_start(
                out=x0_rows[b][:, chunks].rearrange("p h e f -> p (h e f)"),
                in_=x0[b, nodes, :].rearrange("(p t) f -> p (t f)", t=PACK),
            )

        def chunk_rows(array, c):
            g, h = divmod(c, CHUNKS_PER_PASS)
            nodes = slice(g * P * PACK, (g + 1) * P * PACK)
            return array[nodes, :].rearrange("(p h e) k -> h p (e k)", h=CHUNKS_PER_PASS, e=PAIR)[h]

        def load_adj(c):
            nc.sync.dma_start(out=adj_rows[c][:], in_=chunk_rows(adj, c))

        def store(queue, out, rows, b, c):
            queue.dma_start(
                out=chunk_rows(out[b], c),
                in_=rows[b][:, c].rearrange("p e f -> p (e f)"),
            )

        def regroup(copy, grouped, rows, b, g):
            chunks = slice(g * CHUNKS_PER_PASS, (g + 1) * CHUNKS_PER_PASS)
            copy(
                out=grouped[b][:, g].rearrange("p (n i) t -> p n t i", i=RUN),
                in_=rows[b][:, chunks].rearrange("p u e (n i) -> p n (u e) i", i=RUN),
            )

        def quantise(grouped, codes, scales):
            nc.vector.quantize_mx(out=codes.bitcast(FP8X4), scales=scales, in_=grouped)

        def quantise_x0(b, g):
            quantise(x0_grouped[b][:, g].rearrange("p f t -> p (f t)"), x0_codes[b][:, g], x0_scales[b][:, g])

        def transpose_adj(c, e):
            words = adj_rows[c][:].bitcast(F32)
            flipped = psum.tile([P, CHUNKS, P], F32, tag="bank")
            for j in range(CHUNKS):
                g, h = divmod(j, CHUNKS_PER_PASS)
                start = e * WORDS + g * P * CHUNKS_PER_PASS
                stop = start + P * CHUNKS_PER_PASS
                nc.tensor.transpose(flipped[:, j, :], words[:, start + h : stop : CHUNKS_PER_PASS], identity[:])
            return flipped

        def copy_adj(c, e, flipped):
            nc.scalar.copy(
                out=adj_grouped[c][:, e].bitcast(F32).rearrange(
                    "p (g r u) -> p g r u", g=PASSES, u=CHUNKS_PER_PASS
                ),
                in_=flipped[:].rearrange("p (g u) r -> p g r u", u=CHUNKS_PER_PASS),
            )

        def quantise_adj(c, e):
            quantise(
                adj_grouped[c][:, e],
                adj_codes[c][:, e].rearrange("p g r -> p (g r)"),
                adj_scales[c][:, e].rearrange("p g r -> p (g r)"),
            )

        def multiply_zeros(unused):
            nc.tensor.matmul(out=unused[:], lhsT=zeros[:, :P], rhs=zeros[:], start=True, stop=True)

        def multiply(c, codes, scales):
            product = psum.tile([P, PAIR, FEATURES], F32, tag="bank")
            for e in range(PAIR):
                for g in range(PASSES):
                    nc.tensor.matmul_mx(
                        out=product[:, e, :],
                        lhsT=adj_codes[c][:, e, g, :].bitcast(FP8X4),
                        lhsT_scale=adj_scales[c][:, e, g, :],
                        rhs=codes[:, g, :].bitcast(FP8X4),
                        rhs_scale=scales[:, g, :],
                        start=(g == 0),
                        stop=(g == PASSES - 1),
                    )
            return product

        def first_product(b, c):
            product = multiply(c, x0_codes[b], x0_scales[b])
            nc.scalar.copy(out=x1_rows[b][:, c], in_=product[:])
            store(nc.sync, out_0, x1_rows, b, c)

        def quantise_x1(b, g):
            quantise(x1_grouped[b][:, g].rearrange("p f t -> p (f t)"), x1_codes[b][:, g], x1_scales[b][:, g])

        def second_product(b, c):
            product = multiply(c, x1_codes[b], x1_scales[b])
            nc.vector.scalar_tensor_tensor(
                out=x2_rows[b][:, c],
                in0=product[:],
                scalar=2.0,
                in1=x0_rows[b][:, c],
                op0=mybir.AluOpType.mult,
                op1=mybir.AluOpType.subtract,
            )
            store((nc.sync, nc.scalar)[c % 2], out_1, x2_rows, b, c)

        with tc.manual_schedule():
            for g in range(PASSES):
                load_x0(0, g)
            for c in range(CHUNKS):
                load_adj(c)
            for g in range(PASSES):
                load_x0(1, g)
            make_identity(nc, identity[:])

            nc.vector.memset(zeros[:], 0.0)
            unused = psum.tile([P, PACK * P], F32, tag="bank")
            for i in range(WARM_UP):
                multiply_zeros(unused)

            for g in range(PASSES):
                regroup(nc.vector.tensor_copy, x0_grouped, x0_rows, 0, g)
                quantise_x0(0, g)
            for c in range(CHUNKS):
                for e in range(PAIR):
                    copy_adj(c, e, transpose_adj(c, e))
                quantise_adj(c, 0)
                if c >= CHUNKS - PASSES:
                    regroup(nc.vector.tensor_copy, x0_grouped, x0_rows, 1, c - (CHUNKS - PASSES))
                quantise_adj(c, 1)
            for g in range(PASSES):
                quantise_x0(1, g)

            for c in range(CHUNKS):
                first_product(0, c)
            for g in range(PASSES):
                regroup(nc.vector.tensor_copy, x1_grouped, x1_rows, 0, g)
            for g in range(PASSES):
                quantise_x1(0, g)
            for c in range(CHUNKS_PER_PASS):
                first_product(1, c)
            regroup(nc.vector.tensor_copy, x1_grouped, x1_rows, 1, 0)
            for c in range(CHUNKS_PER_PASS, CHUNKS):
                first_product(1, c)
            regroup(nc.scalar.copy, x1_grouped, x1_rows, 1, 1)
            second_product(0, 0)
            quantise_x1(1, 0)
            second_product(0, 1)
            quantise_x1(1, 1)
            for c in range(2, CHUNKS):
                second_product(0, c)
            for c in range(CHUNKS):
                second_product(1, c)
